import numpy as np
import ml_dtypes


def mxq(x, axis, fmt="e4m3"):
    dtype, down = {"e4m3": (ml_dtypes.float8_e4m3fn, 7), "e5m2": (ml_dtypes.float8_e5m2, 14)}[fmt]
    v = np.moveaxis(np.asarray(x, np.float32).astype(ml_dtypes.bfloat16).astype(np.float64), axis, -1)
    blocks = v.reshape(v.shape[:-1] + (-1, 32))
    amax = np.abs(blocks).max(-1, keepdims=True)
    byte = np.maximum(np.where(amax > 0, np.frexp(amax)[1] - 1 + 127, 0) - down, 1)
    scale = np.exp2(byte - 127.0)
    codes = (blocks / scale).astype(np.float32).astype(dtype).astype(np.float64)
    return np.moveaxis((codes * scale).reshape(v.shape), -1, axis)


WIDE = False


def mx_kscale(k):
    if not WIDE:
        return np.ones(k)
    levels = np.array([20, -20, 10, -10, 0])
    a = np.random.permutation(np.resize(levels, k // 512 * 4)).reshape(k // 512, 4)
    idx = np.arange(k)
    return np.exp2(a[idx // 512, idx % 128 // 32])


BF16 = ml_dtypes.bfloat16


def bf(x):
    return np.asarray(x, np.float32).astype(BF16)


def f64(x):
    return np.asarray(x).astype(np.float64)


Nc, Ns, Nt, d_h, BS = 64, 64, 16, 128, 16
I, J = Ns * Nt, Nc * Nt
K = BS * d_h


def setup_inputs():
    s = mx_kscale(K).reshape(BS, 1, 1, d_h)
    Ac = (np.random.random((Ns, Nc)) < 3.2 / Ns).astype(np.float64)
    Ac[np.random.randint(0, Ns, Nc), np.arange(Nc)] = 1.0
    Ac[np.arange(Ns), np.random.randint(0, Nc, Ns)] = 1.0
    As = (np.random.random((Ns, Ns)) < 0.05).astype(np.float64)
    AA = np.dot(np.dot(As, As), Ac) + np.dot(As, Ac) + Ac
    AA = (AA != 0).astype(np.float64)
    AA_mask = bf(np.tile(AA, (Nt, Nt)))
    gain = 1.0 / np.sqrt(0.5 * J * AA.mean())
    GCW = bf(np.random.standard_normal((I, J)) * gain)
    GCB = bf(np.random.standard_normal((I, d_h)) * 0.5)
    h0 = bf(np.random.standard_normal((BS, Nc, Nt, d_h)))
    e = bf(np.random.standard_normal(1) * 0.1)
    g = bf(np.random.standard_normal((BS, Ns, Nt, d_h)) * np.exp2(np.random.randint(-12, 1, (BS, Ns, Nt, 1))) / s)
    A = np.maximum(f64(AA_mask) * f64(GCW), 0.0)
    x0 = np.transpose(f64(h0), (0, 2, 1, 3)).reshape(BS, Nt * Nc, d_h)
    z = A @ x0 + f64(GCB)
    return {"h": bf(f64(h0) * s), "e": e, "AA_mask": AA_mask, "GCW": GCW, "GCB": GCB,
            "z": np.asarray(z, np.float32), "grad_out": g}


def reference(h, e, AA_mask, GCW, GCB, z, grad_out):
    bs = h.shape[0]
    x = np.transpose(f64(h), (2, 1, 0, 3)).reshape(Nt * Nc, bs * d_h)
    g = np.transpose(f64(grad_out), (2, 1, 0, 3)).reshape(Nt * Ns, bs * d_h)
    zz = np.transpose(f64(z), (1, 0, 2)).reshape(Nt * Ns, bs * d_h)
    dz = g * (zz > 0.0)
    dA = mxq(dz, 1, "e5m2") @ mxq(x, 1, "e4m3").T
    m = f64(AA_mask)
    return dA * m * (m * f64(GCW) > 0.0)

@@ -1,0 +1,196 @@
+import concourse.mybir as mybir
+from concourse.masks import make_identity
+
+F32 = mybir.dt.float32
+BF16 = mybir.dt.bfloat16
+U32 = mybir.dt.uint32
+U8 = mybir.dt.uint8
+E4M3_X4 = mybir.dt.float8_e4m3fn_x4
+E5M2_X4 = mybir.dt.float8_e5m2_x4
+ALU = mybir.AluOpType
+
+P = 128
+BATCH = 16
+NODES = 64
+STEPS = 16
+FEAT = 128
+ROWS = NODES * STEPS
+PACK = 4
+B_PASS = 4
+PASSES = BATCH // B_PASS
+HALVES = 2
+R_TILES = STEPS // HALVES
+N_COLS = ROWS // HALVES
+Z_AHEAD = 2
+
+FLOPS = 2 * ROWS * ROWS * BATCH * FEAT
+
+
+def words_by_parity(rows_bf16):
+    return rows_bf16.bitcast(F32).rearrange("p (n q u) -> p n u q", q=P, u=2)
+
+
+def tile_gcnfast_v_kernel(tc, h, e, AA_mask, GCW, GCB, z, grad_out, out):
+    nc = tc.nc
+
+    h_rows = h.rearrange("b c (th r) d -> (c th) b (r d)", th=HALVES)
+    g_rows = grad_out.rearrange("b s (th r) d -> (s th) b (r d)", th=HALVES)
+
+    with (
+        tc.tile_pool(name="keep", bufs=1) as keep,
+        tc.tile_pool(name="x_stage", bufs=2) as x_stage,
+        tc.tile_pool(name="h_stage", bufs=4) as h_stage,
+        tc.tile_pool(name="z_stage", bufs=3) as z_stage,
+        tc.tile_pool(name="dz_stage", bufs=2) as dz_stage,
+        tc.psum_pool(name="flipped", bufs=4) as flipped,
+        tc.psum_pool(name="sums", bufs=4) as sums,
+        tc.manual_schedule(),
+    ):
+        ident = keep.tile([P, P], F32)
+        make_identity(nc, ident[:])
+
+        h_tiles = []
+        for g in range(PASSES):
+            h_t = h_stage.tile([P, B_PASS, R_TILES * FEAT], BF16)
+            nc.sync.dma_start(out=h_t[:], in_=h_rows[:, g * B_PASS : (g + 1) * B_PASS, :])
+            h_tiles.append(h_t)
+        mask_t = keep.tile([P, R_TILES, ROWS], BF16)
+        gcw_t = keep.tile([P, R_TILES, ROWS], BF16)
+        for r0 in range(0, R_TILES, R_TILES // 2):
+            for th in range(HALVES):
+                i0 = (th * R_TILES + r0) * NODES
+                rows = slice(i0, i0 + NODES * R_TILES // 2)
+                tiles = slice(r0, r0 + R_TILES // 2)
+                nc.sync.dma_start(
+                    out=mask_t[th:P:HALVES, tiles, :],
+                    in_=AA_mask[rows, :].rearrange("(r s) j -> s r j", s=NODES),
+                )
+                nc.sync.dma_start(
+                    out=gcw_t[th:P:HALVES, tiles, :],
+                    in_=GCW[rows, :].rearrange("(r s) j -> s r j", s=NODES),
+                )
+        g_t = keep.tile([P, BATCH, R_TILES * FEAT], BF16)
+        for g in range(PASSES):
+            batches = slice(g * B_PASS, (g + 1) * B_PASS)
+            nc.sync.dma_start(out=g_t[:, batches, :], in_=g_rows[:, batches, :])
+
+        x_codes = keep.tile([P, PASSES, ROWS], U32, align_bytes=64)
+        x_scales = keep.tile([P, PASSES, ROWS], U8, align_bytes=64)
+        x_rows_of = {}
+
+        def gather_x_rows(g):
+            x_rows = x_stage.tile([P, R_TILES * B_PASS * FEAT], BF16)
+            nc.vector.tensor_copy(
+                out=x_rows[:].rearrange("p (r b d) -> p r b d", r=R_TILES, b=B_PASS),
+                in_=h_tiles[g][:].rearrange("p b (r d) -> p r b d", r=R_TILES),
+            )
+            x_rows_of[g] = x_rows
+
+        gather_x_rows(0)
+        for g in range(PASSES):
+            if g + 1 < PASSES:
+                gather_x_rows(g + 1)
+            x_words = words_by_parity(x_rows_of[g][:])
+            x_grouped = x_stage.tile([P, HALVES, N_COLS, PACK], BF16, align_bytes=64)
+            for r0 in range(0, R_TILES, 2):
+                x_flip = flipped.tile([P, 2, 2, P], F32, tag="flip")
+                for u in range(2):
+                    for rr in range(2):
+                        nc.tensor.transpose(x_flip[:, u, rr, :], x_words[:, r0 + rr, u, :], ident[:])
+                nc.scalar.copy(
+                    out=x_grouped[:].bitcast(F32)[:, :, r0 * NODES : (r0 + 2) * NODES, :],
+                    in_=x_flip[:].rearrange("k u rr (c th) -> k th (rr c) u", th=HALVES),
+                )
+            nc.vector.quantize_mx(
+                out=x_codes[:, g, :].bitcast(E4M3_X4),
+                scales=x_scales[:, g, :],
+                in_=x_grouped[:].rearrange("k th j t -> k (th j t)"),
+            )
+
+        gate = keep.tile([P, R_TILES, ROWS], BF16)
+        for r in range(R_TILES):
+            product = dz_stage.tile([P, ROWS], F32)
+            nc.vector.tensor_tensor(out=product[:], in0=mask_t[:, r, :], in1=gcw_t[:, r, :], op=ALU.mult)
+            nc.vector.scalar_tensor_tensor(
+                out=gate[:, r, :], in0=product[:], scalar=0.0, in1=mask_t[:, r, :],
+                op0=ALU.is_gt, op1=ALU.mult,
+            )
+
+        z_of, grouped_of, sums_of = {}, {}, {}
+
+        def load_z(r):
+            z_t = z_stage.tile([P, BATCH, FEAT], F32)
+            for th in range(HALVES):
+                i0 = (th * R_TILES + r) * NODES
+                nc.sync.dma_start(
+                    out=z_t[th:P:HALVES, :, :],
+                    in_=z[:, i0 : i0 + NODES, :].rearrange("b s d -> s b d"),
+                )
+            z_of[r] = z_t
+
+        def mask_and_flip(r):
+            dz_rows = dz_stage.tile([P, BATCH, FEAT], BF16)
+            nc.vector.scalar_tensor_tensor(
+                out=dz_rows[:], in0=z_of[r][:], scalar=0.0, in1=g_t[:, :, r * FEAT : (r + 1) * FEAT],
+                op0=ALU.is_gt, op1=ALU.mult,
+            )
+            dz_words = words_by_parity(dz_rows[:].rearrange("p b d -> p (b d)"))
+            dz_grouped = dz_stage.tile([P, PASSES, P, PACK], BF16, align_bytes=64)
+            for g0 in range(0, PASSES, 2):
+                dz_flip = flipped.tile([P, 2, 2, P], F32, tag="flip")
+                for gg in range(2):
+                    for u in range(2):
+                        nc.tensor.transpose(dz_flip[:, gg, u, :], dz_words[:, g0 + gg, u, :], ident[:])
+                nc.scalar.copy(
+                    out=dz_grouped[:].bitcast(F32)[:, g0 : g0 + 2, :, :],
+                    in_=dz_flip[:].rearrange("k gg u m -> k gg m u"),
+                )
+            grouped_of[r] = dz_grouped
+
+        def quantise_and_multiply(r):
+            dz_codes = dz_stage.tile([P, PASSES * P], U32, align_bytes=64)
+            dz_scales = dz_stage.tile([P, PASSES * P], U8, align_bytes=64)
+            nc.vector.quantize_mx(
+                out=dz_codes[:].bitcast(E5M2_X4),
+                scales=dz_scales[:],
+                in_=grouped_of[r][:].rearrange("k g m t -> k (g m t)"),
+            )
+            sums_of[r] = []
+            for n in range(HALVES):
+                cols = slice(n * N_COLS, (n + 1) * N_COLS)
+                acc = sums.tile([P, N_COLS], F32)
+                for g in range(PASSES):
+                    m_cols = slice(g * P, (g + 1) * P)
+                    nc.tensor.matmul_mx(
+                        out=acc[:],
+                        lhsT=dz_codes[:, m_cols].bitcast(E5M2_X4),
+                        lhsT_scale=dz_scales[:, m_cols],
+                        rhs=x_codes[:, g, cols].bitcast(E4M3_X4),
+                        rhs_scale=x_scales[:, g, cols],
+                        start=(g == 0),
+                        stop=(g == PASSES - 1),
+                    )
+                sums_of[r].append(acc)
+
+        def gate_and_store(r):
+            out_t = dz_stage.tile([P, ROWS], F32)
+            for n in range(HALVES):
+                cols = slice(n * N_COLS, (n + 1) * N_COLS)
+                nc.vector.tensor_tensor(
+                    out=out_t[:, cols], in0=sums_of[r][n][:], in1=gate[:, r, cols], op=ALU.mult
+                )
+            for th in range(HALVES):
+                i0 = (th * R_TILES + r) * NODES
+                nc.gpsimd.dma_start(out=out[i0 : i0 + NODES, :], in_=out_t[th:P:HALVES, :])
+
+        for r in range(Z_AHEAD):
+            load_z(r)
+        for r in range(R_TILES + 2):
+            if r + Z_AHEAD < R_TILES:
+                load_z(r + Z_AHEAD)
+            if r < R_TILES:
+                mask_and_flip(r)
+            if 1 <= r <= R_TILES:
+                quantise_and_multiply(r - 1)
+            if r >= 2:
+                gate_and_store(r - 2)

@@ -42,6 +42,7 @@ def tile_gcnfast_v_kernel(tc, h, e, AA_mask, GCW, GCB, z, grad_out, out):
         tc.tile_pool(name="h_stage", bufs=4) as h_stage,
         tc.tile_pool(name="z_stage", bufs=3) as z_stage,
         tc.tile_pool(name="dz_stage", bufs=2) as dz_stage,
+        tc.tile_pool(name="out_stage", bufs=3) as out_stage,
         tc.psum_pool(name="flipped", bufs=4) as flipped,
         tc.psum_pool(name="sums", bufs=4) as sums,
         tc.manual_schedule(),
@@ -49,14 +50,10 @@ def tile_gcnfast_v_kernel(tc, h, e, AA_mask, GCW, GCB, z, grad_out, out):
         ident = keep.tile([P, P], F32)
         make_identity(nc, ident[:])
 
-        h_tiles = []
-        for g in range(PASSES):
-            h_t = h_stage.tile([P, B_PASS, R_TILES * FEAT], BF16)
-            nc.sync.dma_start(out=h_t[:], in_=h_rows[:, g * B_PASS : (g + 1) * B_PASS, :])
-            h_tiles.append(h_t)
         mask_t = keep.tile([P, R_TILES, ROWS], BF16)
         gcw_t = keep.tile([P, R_TILES, ROWS], BF16)
-        for r0 in range(0, R_TILES, R_TILES // 2):
+
+        def load_mask_and_gcw(r0):
             for th in range(HALVES):
                 i0 = (th * R_TILES + r0) * NODES
                 rows = slice(i0, i0 + NODES * R_TILES // 2)
@@ -69,6 +66,14 @@ def tile_gcnfast_v_kernel(tc, h, e, AA_mask, GCW, GCB, z, grad_out, out):
                     out=gcw_t[th:P:HALVES, tiles, :],
                     in_=GCW[rows, :].rearrange("(r s) j -> s r j", s=NODES),
                 )
+
+        load_mask_and_gcw(0)
+        h_tiles = []
+        for g in range(PASSES):
+            h_t = h_stage.tile([P, B_PASS, R_TILES * FEAT], BF16)
+            nc.sync.dma_start(out=h_t[:], in_=h_rows[:, g * B_PASS : (g + 1) * B_PASS, :])
+            h_tiles.append(h_t)
+        load_mask_and_gcw(R_TILES // 2)
         g_t = keep.tile([P, BATCH, R_TILES * FEAT], BF16)
         for g in range(PASSES):
             batches = slice(g * B_PASS, (g + 1) * B_PASS)
@@ -76,15 +81,24 @@ def tile_gcnfast_v_kernel(tc, h, e, AA_mask, GCW, GCB, z, grad_out, out):
 
         x_codes = keep.tile([P, PASSES, ROWS], U32, align_bytes=64)
         x_scales = keep.tile([P, PASSES, ROWS], U8, align_bytes=64)
+        gate = keep.tile([P, R_TILES, ROWS], BF16)
         x_rows_of = {}
 
         def gather_x_rows(g):
             x_rows = x_stage.tile([P, R_TILES * B_PASS * FEAT], BF16)
-            nc.vector.tensor_copy(
-                out=x_rows[:].rearrange("p (r b d) -> p r b d", r=R_TILES, b=B_PASS),
-                in_=h_tiles[g][:].rearrange("p b (r d) -> p r b d", r=R_TILES),
+            nc.scalar.copy(
+                out=x_rows[:].bitcast(F32).rearrange("p (r b w) -> p r b w", r=R_TILES, b=B_PASS),
+                in_=h_tiles[g][:].bitcast(F32).rearrange("p b (r w) -> p r b w", r=R_TILES),
             )
             x_rows_of[g] = x_rows
+
+        def make_gate(r):
+            product = dz_stage.tile([P, ROWS], F32)
+            nc.vector.tensor_tensor(out=product[:], in0=mask_t[:, r, :], in1=gcw_t[:, r, :], op=ALU.mult)
+            nc.vector.scalar_tensor_tensor(
+                out=gate[:, r, :], in0=product[:], scalar=0.0, in1=mask_t[:, r, :],
+                op0=ALU.is_gt, op1=ALU.mult,
+            )
 
         gather_x_rows(0)
         for g in range(PASSES):
@@ -101,19 +115,12 @@ def tile_gcnfast_v_kernel(tc, h, e, AA_mask, GCW, GCB, z, grad_out, out):
                     out=x_grouped[:].bitcast(F32)[:, :, r0 * NODES : (r0 + 2) * NODES, :],
                     in_=x_flip[:].rearrange("k u rr (c th) -> k th (rr c) u", th=HALVES),
                 )
+            for r in range(g * R_TILES // PASSES, (g + 1) * R_TILES // PASSES):
+                make_gate(r)
             nc.vector.quantize_mx(
                 out=x_codes[:, g, :].bitcast(E4M3_X4),
                 scales=x_scales[:, g, :],
                 in_=x_grouped[:].rearrange("k th j t -> k (th j t)"),
-            )
-
-        gate = keep.tile([P, R_TILES, ROWS], BF16)
-        for r in range(R_TILES):
-            product = dz_stage.tile([P, ROWS], F32)
-            nc.vector.tensor_tensor(out=product[:], in0=mask_t[:, r, :], in1=gcw_t[:, r, :], op=ALU.mult)
-            nc.vector.scalar_tensor_tensor(
-                out=gate[:, r, :], in0=product[:], scalar=0.0, in1=mask_t[:, r, :],
-                op0=ALU.is_gt, op1=ALU.mult,
             )
 
         z_of, grouped_of, sums_of = {}, {}, {}
@@ -173,7 +180,7 @@ def tile_gcnfast_v_kernel(tc, h, e, AA_mask, GCW, GCB, z, grad_out, out):
                 sums_of[r].append(acc)
 
         def gate_and_store(r):
-            out_t = dz_stage.tile([P, ROWS], F32)
+            out_t = out_stage.tile([P, ROWS], F32)
             for n in range(HALVES):
                 cols = slice(n * N_COLS, (n + 1) * N_COLS)
                 nc.vector.tensor_tensor(
@@ -181,7 +188,7 @@ def tile_gcnfast_v_kernel(tc, h, e, AA_mask, GCW, GCB, z, grad_out, out):
                 )
             for th in range(HALVES):
                 i0 = (th * R_TILES + r) * NODES
-                nc.gpsimd.dma_start(out=out[i0 : i0 + NODES, :], in_=out_t[th:P:HALVES, :])
+                nc.scalar.dma_start(out=out[i0 : i0 + NODES, :], in_=out_t[th:P:HALVES, :])
 
         for r in range(Z_AHEAD):
             load_z(r)

@@ -93,7 +93,7 @@ def tile_gcnfast_v_kernel(tc, h, e, AA_mask, GCW, GCB, z, grad_out, out):
             x_rows_of[g] = x_rows
 
         def make_gate(r):
-            product = dz_stage.tile([P, ROWS], F32)
+            product = dz_stage.tile([P, ROWS], BF16)
             nc.vector.tensor_tensor(out=product[:], in0=mask_t[:, r, :], in1=gcw_t[:, r, :], op=ALU.mult)
             nc.vector.scalar_tensor_tensor(
                 out=gate[:, r, :], in0=product[:], scalar=0.0, in1=mask_t[:, r, :],

@@ -8,6 +8,7 @@ U8 = mybir.dt.uint8
 E4M3_X4 = mybir.dt.float8_e4m3fn_x4
 E5M2_X4 = mybir.dt.float8_e5m2_x4
 ALU = mybir.AluOpType
+ACT = mybir.ActivationFunctionType
 
 P = 128
 BATCH = 16
@@ -16,152 +17,190 @@ STEPS = 16
 FEAT = 128
 ROWS = NODES * STEPS
 PACK = 4
-B_PASS = 4
-PASSES = BATCH // B_PASS
-HALVES = 2
-R_TILES = STEPS // HALVES
-N_COLS = ROWS // HALVES
-Z_AHEAD = 2
+PASSES = BATCH // PACK
+PAIRS = BATCH // 2
+TILES = ROWS // P
+N_COLS = 512
+HALVES = ROWS // N_COLS
+BANK = 8
+Z_BUFS = 4
+MG_BUFS = 4
+QUARTER = STEPS // 4
 
 FLOPS = 2 * ROWS * ROWS * BATCH * FEAT
-
-
-def words_by_parity(rows_bf16):
-    return rows_bf16.bitcast(F32).rearrange("p (n q u) -> p n u q", q=P, u=2)
 
 
 def tile_gcnfast_v_kernel(tc, h, e, AA_mask, GCW, GCB, z, grad_out, out):
     nc = tc.nc
 
-    h_rows = h.rearrange("b c (th r) d -> (c th) b (r d)", th=HALVES)
-    g_rows = grad_out.rearrange("b s (th r) d -> (s th) b (r d)", th=HALVES)
-
     with (
         tc.tile_pool(name="keep", bufs=1) as keep,
+        tc.tile_pool(name="h_stage", bufs=PASSES) as h_stage,
         tc.tile_pool(name="x_stage", bufs=2) as x_stage,
-        tc.tile_pool(name="h_stage", bufs=4) as h_stage,
-        tc.tile_pool(name="z_stage", bufs=3) as z_stage,
+        tc.tile_pool(name="z_stage", bufs=Z_BUFS) as z_stage,
+        tc.tile_pool(name="mg_stage", bufs=MG_BUFS) as mg_stage,
         tc.tile_pool(name="dz_stage", bufs=2) as dz_stage,
         tc.tile_pool(name="out_stage", bufs=3) as out_stage,
         tc.psum_pool(name="flipped", bufs=4) as flipped,
         tc.psum_pool(name="sums", bufs=4) as sums,
         tc.manual_schedule(),
     ):
-        ident = keep.tile([P, P], F32)
+        ident = keep.tile([P, P], BF16)
         make_identity(nc, ident[:])
+        warm = keep.tile([P, 1], BF16)
+        nc.scalar.activation(out=warm[:], in_=ident[:, 0:1], func=ACT.Sign)
 
-        mask_t = keep.tile([P, R_TILES, ROWS], BF16)
-        gcw_t = keep.tile([P, R_TILES, ROWS], BF16)
-
-        def load_mask_and_gcw(r0):
-            for th in range(HALVES):
-                i0 = (th * R_TILES + r0) * NODES
-                rows = slice(i0, i0 + NODES * R_TILES // 2)
-                tiles = slice(r0, r0 + R_TILES // 2)
-                nc.sync.dma_start(
-                    out=mask_t[th:P:HALVES, tiles, :],
-                    in_=AA_mask[rows, :].rearrange("(r s) j -> s r j", s=NODES),
-                )
-                nc.sync.dma_start(
-                    out=gcw_t[th:P:HALVES, tiles, :],
-                    in_=GCW[rows, :].rearrange("(r s) j -> s r j", s=NODES),
-                )
-
-        load_mask_and_gcw(0)
         h_tiles = []
         for g in range(PASSES):
-            h_t = h_stage.tile([P, B_PASS, R_TILES * FEAT], BF16)
-            nc.sync.dma_start(out=h_t[:], in_=h_rows[:, g * B_PASS : (g + 1) * B_PASS, :])
-            h_tiles.append(h_t)
-        load_mask_and_gcw(R_TILES // 2)
-        g_t = keep.tile([P, BATCH, R_TILES * FEAT], BF16)
-        for g in range(PASSES):
-            batches = slice(g * B_PASS, (g + 1) * B_PASS)
-            nc.sync.dma_start(out=g_t[:, batches, :], in_=g_rows[:, batches, :])
+            h_g = h_stage.tile([P, 2, STEPS, FEAT], BF16)
+            for b1 in range(2):
+                nc.sync.dma_start(
+                    out=h_g[b1:P:2, :, :, :].rearrange("c b2 t d -> c b2 (t d)"),
+                    in_=h[PACK * g + b1 : PACK * (g + 1) : 2, :, :, :].rearrange("b2 c t d -> c b2 (t d)"),
+                )
+            h_tiles.append(h_g)
+
+        g_of, z_of, mask_of, gcw_of = {}, {}, {}, {}
+
+        def load_g(q):
+            g_q = keep.tile([P, PAIRS, QUARTER, FEAT], BF16, name="g_q%d" % q)
+            for b1 in range(2):
+                nc.sync.dma_start(
+                    out=g_q[b1:P:2, :, :, :].rearrange("s bh tq d -> s bh (tq d)"),
+                    in_=grad_out[b1:BATCH:2, :, q * QUARTER : (q + 1) * QUARTER, :].rearrange(
+                        "bh s tq d -> s bh (tq d)"
+                    ),
+                )
+            g_of[q] = g_q
+
+        def load_z(r):
+            z_t = z_stage.tile([P, 2, PAIRS, FEAT], F32)
+            for tau in range(2):
+                i0 = (2 * r + tau) * NODES
+                for b1 in range(2):
+                    nc.sync.dma_start(
+                        out=z_t[b1:P:2, tau, :, :],
+                        in_=z[b1:BATCH:2, i0 : i0 + NODES, :].rearrange("bh s d -> s bh d"),
+                    )
+            z_of[r] = z_t
+
+        def load_mask_and_gcw(r):
+            mask_t = mg_stage.tile([P, ROWS], BF16)
+            gcw_t = mg_stage.tile([P, ROWS], BF16)
+            nc.sync.dma_start(out=mask_t[:], in_=AA_mask[r * P : (r + 1) * P, :])
+            nc.sync.dma_start(out=gcw_t[:], in_=GCW[r * P : (r + 1) * P, :])
+            mask_of[r], gcw_of[r] = mask_t, gcw_t
+
+        load_g(0)
+        load_z(0)
+        load_z(1)
+        load_mask_and_gcw(0)
+        load_g(1)
+        load_z(2)
+        load_mask_and_gcw(1)
+        load_z(3)
+        load_mask_and_gcw(2)
 
         x_codes = keep.tile([P, PASSES, ROWS], U32, align_bytes=64)
         x_scales = keep.tile([P, PASSES, ROWS], U8, align_bytes=64)
-        gate = keep.tile([P, R_TILES, ROWS], BF16)
-        x_rows_of = {}
+        x_grouped_of = {}
 
-        def gather_x_rows(g):
-            x_rows = x_stage.tile([P, R_TILES * B_PASS * FEAT], BF16)
-            nc.scalar.copy(
-                out=x_rows[:].bitcast(F32).rearrange("p (r b w) -> p r b w", r=R_TILES, b=B_PASS),
-                in_=h_tiles[g][:].bitcast(F32).rearrange("p b (r w) -> p r b w", r=R_TILES),
-            )
-            x_rows_of[g] = x_rows
-
-        def make_gate(r):
-            product = dz_stage.tile([P, ROWS], BF16)
-            nc.vector.tensor_tensor(out=product[:], in0=mask_t[:, r, :], in1=gcw_t[:, r, :], op=ALU.mult)
-            nc.vector.scalar_tensor_tensor(
-                out=gate[:, r, :], in0=product[:], scalar=0.0, in1=mask_t[:, r, :],
-                op0=ALU.is_gt, op1=ALU.mult,
-            )
-
-        gather_x_rows(0)
-        for g in range(PASSES):
-            if g + 1 < PASSES:
-                gather_x_rows(g + 1)
-            x_words = words_by_parity(x_rows_of[g][:])
-            x_grouped = x_stage.tile([P, HALVES, N_COLS, PACK], BF16, align_bytes=64)
-            for r0 in range(0, R_TILES, 2):
-                x_flip = flipped.tile([P, 2, 2, P], F32, tag="flip")
-                for u in range(2):
-                    for rr in range(2):
-                        nc.tensor.transpose(x_flip[:, u, rr, :], x_words[:, r0 + rr, u, :], ident[:])
-                nc.scalar.copy(
-                    out=x_grouped[:].bitcast(F32)[:, :, r0 * NODES : (r0 + 2) * NODES, :],
-                    in_=x_flip[:].rearrange("k u rr (c th) -> k th (rr c) u", th=HALVES),
-                )
-            for r in range(g * R_TILES // PASSES, (g + 1) * R_TILES // PASSES):
-                make_gate(r)
+        def quantise_x(g):
             nc.vector.quantize_mx(
                 out=x_codes[:, g, :].bitcast(E4M3_X4),
                 scales=x_scales[:, g, :],
-                in_=x_grouped[:].rearrange("k th j t -> k (th j t)"),
+                in_=x_grouped_of[g][:],
             )
 
-        z_of, grouped_of, sums_of = {}, {}, {}
-
-        def load_z(r):
-            z_t = z_stage.tile([P, BATCH, FEAT], F32)
-            for th in range(HALVES):
-                i0 = (th * R_TILES + r) * NODES
-                nc.sync.dma_start(
-                    out=z_t[th:P:HALVES, :, :],
-                    in_=z[:, i0 : i0 + NODES, :].rearrange("b s d -> s b d"),
+        T_BANK = BANK // 2
+        for g in range(PASSES):
+            x_grouped = x_stage.tile([P, ROWS * PACK], BF16, align_bytes=64)
+            x_grouped_of[g] = x_grouped
+            for t0 in range(0, STEPS, T_BANK):
+                x_flip = flipped.tile([P, T_BANK, 2, P], BF16, tag="flip")
+                for tt in range(T_BANK):
+                    for b2 in range(2):
+                        nc.tensor.transpose(x_flip[:, tt, b2, :], h_tiles[g][:, b2, t0 + tt, :], ident[:])
+                src = (
+                    x_flip[:]
+                    .rearrange("k t b2 n -> k (t b2 n)")
+                    .bitcast(F32)
+                    .rearrange("k (t b2 c) -> k t c b2", t=T_BANK, b2=2)
                 )
-            z_of[r] = z_t
+                dst = (
+                    x_grouped[:, t0 * NODES * PACK : (t0 + T_BANK) * NODES * PACK]
+                    .bitcast(F32)
+                    .rearrange("k (t c b2) -> k t c b2", t=T_BANK, b2=2)
+                )
+                if (t0 // T_BANK) % 2 == 0:
+                    nc.scalar.copy(out=dst, in_=src)
+                else:
+                    nc.vector.tensor_copy(out=dst, in_=src)
+                if t0 == T_BANK and g >= 1:
+                    quantise_x(g - 1)
+        quantise_x(PASSES - 1)
 
-        def mask_and_flip(r):
-            dz_rows = dz_stage.tile([P, BATCH, FEAT], BF16)
-            nc.vector.scalar_tensor_tensor(
-                out=dz_rows[:], in0=z_of[r][:], scalar=0.0, in1=g_t[:, :, r * FEAT : (r + 1) * FEAT],
-                op0=ALU.is_gt, op1=ALU.mult,
+        sign_of, rows_of, flip_of, grouped_of, codes_of, sums_of, prod_of, out_of = {}, {}, {}, {}, {}, {}, {}, {}
+
+        def sign(r):
+            sign_t = dz_stage.tile([P, 2, PAIRS, FEAT], BF16)
+            sign_of[r] = sign_t
+            for tau in range(2):
+                nc.scalar.activation(out=sign_t[:, tau, :, :], in_=z_of[r][:, tau, :, :], func=ACT.Sign)
+            if r + Z_BUFS < TILES:
+                if (r + Z_BUFS) % 2 == 0:
+                    load_g((r + Z_BUFS) // 2)
+                load_z(r + Z_BUFS)
+
+        def positive(r, tau):
+            nc.vector.tensor_scalar_max(
+                out=sign_of[r][:, tau, :, :], in0=sign_of[r][:, tau, :, :], scalar1=0.0
             )
-            dz_words = words_by_parity(dz_rows[:].rearrange("p b d -> p (b d)"))
-            dz_grouped = dz_stage.tile([P, PASSES, P, PACK], BF16, align_bytes=64)
-            for g0 in range(0, PASSES, 2):
-                dz_flip = flipped.tile([P, 2, 2, P], F32, tag="flip")
-                for gg in range(2):
-                    for u in range(2):
-                        nc.tensor.transpose(dz_flip[:, gg, u, :], dz_words[:, g0 + gg, u, :], ident[:])
-                nc.scalar.copy(
-                    out=dz_grouped[:].bitcast(F32)[:, g0 : g0 + 2, :, :],
-                    in_=dz_flip[:].rearrange("k gg u m -> k gg m u"),
-                )
-            grouped_of[r] = dz_grouped
 
-        def quantise_and_multiply(r):
+        def mask_rows(r, tau):
+            if tau == 0:
+                dz_rows = dz_stage.tile([P, 2, PAIRS, FEAT], BF16)
+                rows_of[r] = dz_rows
+            nc.vector.tensor_tensor(
+                out=rows_of[r][:, tau, :, :],
+                in0=sign_of[r][:, tau, :, :],
+                in1=g_of[r // 2][:, :, 2 * (r % 2) + tau, :],
+                op=ALU.mult,
+            )
+
+        def flip(r, tau):
+            dz_flip = flipped.tile([P, PAIRS, P], BF16, tag="flip")
+            for bh in range(PAIRS):
+                nc.tensor.transpose(dz_flip[:, bh, :], rows_of[r][:, tau, bh, :], ident[:])
+            flip_of[(r, tau)] = dz_flip
+
+        def regroup(r, tau):
+            if tau == 0:
+                dz_grouped = dz_stage.tile([P, PASSES, P * PACK], BF16, align_bytes=64)
+                grouped_of[r] = dz_grouped
+            words = NODES * 2
+            nc.scalar.copy(
+                out=grouped_of[r][:]
+                .bitcast(F32)[:, :, tau * words : (tau + 1) * words]
+                .rearrange("k g (s b2) -> k g s b2", b2=2),
+                in_=flip_of[(r, tau)][:]
+                .rearrange("k bh n -> k (bh n)")
+                .bitcast(F32)
+                .rearrange("k (g b2 s) -> k g s b2", g=PASSES, b2=2),
+            )
+
+        def quantise(r):
             dz_codes = dz_stage.tile([P, PASSES * P], U32, align_bytes=64)
             dz_scales = dz_stage.tile([P, PASSES * P], U8, align_bytes=64)
             nc.vector.quantize_mx(
                 out=dz_codes[:].bitcast(E5M2_X4),
                 scales=dz_scales[:],
-                in_=grouped_of[r][:].rearrange("k g m t -> k (g m t)"),
+                in_=grouped_of[r][:].rearrange("k g m -> k (g m)"),
             )
+            codes_of[r] = (dz_codes, dz_scales)
+
+        def multiply(r):
+            dz_codes, dz_scales = codes_of[r]
             sums_of[r] = []
             for n in range(HALVES):
                 cols = slice(n * N_COLS, (n + 1) * N_COLS)
@@ -179,25 +218,62 @@ def tile_gcnfast_v_kernel(tc, h, e, AA_mask, GCW, GCB, z, grad_out, out):
                     )
                 sums_of[r].append(acc)
 
-        def gate_and_store(r):
-            out_t = out_stage.tile([P, ROWS], F32)
-            for n in range(HALVES):
-                cols = slice(n * N_COLS, (n + 1) * N_COLS)
-                nc.vector.tensor_tensor(
-                    out=out_t[:, cols], in0=sums_of[r][n][:], in1=gate[:, r, cols], op=ALU.mult
-                )
-            for th in range(HALVES):
-                i0 = (th * R_TILES + r) * NODES
-                nc.scalar.dma_start(out=out[i0 : i0 + NODES, :], in_=out_t[th:P:HALVES, :])
+        def gate_product(r):
+            product = out_stage.tile([P, ROWS], BF16)
+            nc.vector.tensor_tensor(out=product[:], in0=mask_of[r][:], in1=gcw_of[r][:], op=ALU.mult)
+            prod_of[r] = product
+            if r + MG_BUFS < TILES:
+                load_mask_and_gcw(r + MG_BUFS)
 
-        for r in range(Z_AHEAD):
-            load_z(r)
-        for r in range(R_TILES + 2):
-            if r + Z_AHEAD < R_TILES:
-                load_z(r + Z_AHEAD)
-            if r < R_TILES:
-                mask_and_flip(r)
-            if 1 <= r <= R_TILES:
-                quantise_and_multiply(r - 1)
-            if r >= 2:
-                gate_and_store(r - 2)
+        def gate_out(r, n):
+            if n == 0:
+                out_t = out_stage.tile([P, ROWS], F32)
+                out_of[r] = out_t
+            cols = slice(n * N_COLS, (n + 1) * N_COLS)
+            nc.vector.scalar_tensor_tensor(
+                out=out_of[r][:, cols], in0=prod_of[r][:, cols], scalar=0.0, in1=sums_of[r][n][:],
+                op0=ALU.is_gt, op1=ALU.mult,
+            )
+
+        def store(r, n0, n1):
+            cols = slice(n0 * N_COLS, n1 * N_COLS)
+            nc.scalar.dma_start(out=out[r * P : (r + 1) * P, cols], in_=out_of[r][:, cols])
+
+        sign(0)
+        load_mask_and_gcw(3)
+        for tau in range(2):
+            positive(0, tau)
+        for tau in range(2):
+            mask_rows(0, tau)
+        sign(1)
+        for R in range(TILES + 2):
+            if 1 <= R <= TILES:
+                quantise(R - 1)
+            if R < TILES:
+                flip(R, 0)
+                flip(R, 1)
+            if 1 <= R <= TILES:
+                multiply(R - 1)
+            if R + 2 < TILES:
+                sign(R + 2)
+            if R < TILES:
+                regroup(R, 0)
+                regroup(R, 1)
+            if R + 1 < TILES:
+                positive(R + 1, 0)
+                positive(R + 1, 1)
+            if R >= 2:
+                gate_out(R - 2, 0)
+                if R - 2 == TILES - 1:
+                    store(R - 2, 0, 1)
+            if R + 1 < TILES:
+                mask_rows(R + 1, 0)
+                mask_rows(R + 1, 1)
+            if R >= 2:
+                gate_out(R - 2, 1)
+                if R - 2 == TILES - 1:
+                    store(R - 2, 1, 2)
+                else:
+                    store(R - 2, 0, 2)
+            if R < TILES:
+                gate_product(R)

@@ -53,10 +53,11 @@ def tile_gcnfast_v_kernel(tc, h, e, AA_mask, GCW, GCB, z, grad_out, out):
         h_tiles = []
         for g in range(PASSES):
             h_g = h_stage.tile([P, 2, STEPS, FEAT], BF16)
-            for b1 in range(2):
+            for bl in range(PACK):
+                b = PACK * g + bl
                 nc.sync.dma_start(
-                    out=h_g[b1:P:2, :, :, :].rearrange("c b2 t d -> c b2 (t d)"),
-                    in_=h[PACK * g + b1 : PACK * (g + 1) : 2, :, :, :].rearrange("b2 c t d -> c b2 (t d)"),
+                    out=h_g[bl:P:PACK, :, :, :].rearrange("cl ch t d -> cl ch (t d)"),
+                    in_=h[b : b + 1, :, :, :].rearrange("o (ch cl) t d -> cl (o ch) (t d)", ch=2),
                 )
             h_tiles.append(h_g)
 
@@ -119,19 +120,10 @@ def tile_gcnfast_v_kernel(tc, h, e, AA_mask, GCW, GCB, z, grad_out, out):
             for t0 in range(0, STEPS, T_BANK):
                 x_flip = flipped.tile([P, T_BANK, 2, P], BF16, tag="flip")
                 for tt in range(T_BANK):
-                    for b2 in range(2):
-                        nc.tensor.transpose(x_flip[:, tt, b2, :], h_tiles[g][:, b2, t0 + tt, :], ident[:])
-                src = (
-                    x_flip[:]
-                    .rearrange("k t b2 n -> k (t b2 n)")
-                    .bitcast(F32)
-                    .rearrange("k (t b2 c) -> k t c b2", t=T_BANK, b2=2)
-                )
-                dst = (
-                    x_grouped[:, t0 * NODES * PACK : (t0 + T_BANK) * NODES * PACK]
-                    .bitcast(F32)
-                    .rearrange("k (t c b2) -> k t c b2", t=T_BANK, b2=2)
-                )
+                    for ch in range(2):
+                        nc.tensor.transpose(x_flip[:, tt, ch, :], h_tiles[g][:, ch, t0 + tt, :], ident[:])
+                src = x_flip[:].rearrange("k t ch n -> k (t ch n)").bitcast(F32)
+                dst = x_grouped[:, t0 * NODES * PACK : (t0 + T_BANK) * NODES * PACK].bitcast(F32)
                 if (t0 // T_BANK) % 2 == 0:
                     nc.scalar.copy(out=dst, in_=src)
                 else:

@@ -24,8 +24,10 @@ N_COLS = 512
 HALVES = ROWS // N_COLS
 BANK = 8
 Z_BUFS = 4
-MG_BUFS = 4
+MG_BUFS = 8
+MG_EARLY = 4
 QUARTER = STEPS // 4
+STORE_LAG = 2
 
 FLOPS = 2 * ROWS * ROWS * BATCH * FEAT
 
@@ -40,7 +42,8 @@ def tile_gcnfast_v_kernel(tc, h, e, AA_mask, GCW, GCB, z, grad_out, out):
         tc.tile_pool(name="z_stage", bufs=Z_BUFS) as z_stage,
         tc.tile_pool(name="mg_stage", bufs=MG_BUFS) as mg_stage,
         tc.tile_pool(name="dz_stage", bufs=2) as dz_stage,
-        tc.tile_pool(name="out_stage", bufs=3) as out_stage,
+        tc.tile_pool(name="prod_stage", bufs=3) as prod_stage,
+        tc.tile_pool(name="out_stage", bufs=3 + STORE_LAG) as out_stage,
         tc.psum_pool(name="flipped", bufs=4) as flipped,
         tc.psum_pool(name="sums", bufs=4) as sums,
         tc.manual_schedule(),
@@ -95,42 +98,10 @@ def tile_gcnfast_v_kernel(tc, h, e, AA_mask, GCW, GCB, z, grad_out, out):
         load_g(0)
         load_z(0)
         load_z(1)
-        load_mask_and_gcw(0)
         load_g(1)
         load_z(2)
-        load_mask_and_gcw(1)
         load_z(3)
-        load_mask_and_gcw(2)
-
-        x_codes = keep.tile([P, PASSES, ROWS], U32, align_bytes=64)
-        x_scales = keep.tile([P, PASSES, ROWS], U8, align_bytes=64)
-        x_grouped_of = {}
-
-        def quantise_x(g):
-            nc.vector.quantize_mx(
-                out=x_codes[:, g, :].bitcast(E4M3_X4),
-                scales=x_scales[:, g, :],
-                in_=x_grouped_of[g][:],
-            )
-
-        T_BANK = BANK // 2
-        for g in range(PASSES):
-            x_grouped = x_stage.tile([P, ROWS * PACK], BF16, align_bytes=64)
-            x_grouped_of[g] = x_grouped
-            for t0 in range(0, STEPS, T_BANK):
-                x_flip = flipped.tile([P, T_BANK, 2, P], BF16, tag="flip")
-                for tt in range(T_BANK):
-                    for ch in range(2):
-                        nc.tensor.transpose(x_flip[:, tt, ch, :], h_tiles[g][:, ch, t0 + tt, :], ident[:])
-                src = x_flip[:].rearrange("k t ch n -> k (t ch n)").bitcast(F32)
-                dst = x_grouped[:, t0 * NODES * PACK : (t0 + T_BANK) * NODES * PACK].bitcast(F32)
-                if (t0 // T_BANK) % 2 == 0:
-                    nc.scalar.copy(out=dst, in_=src)
-                else:
-                    nc.vector.tensor_copy(out=dst, in_=src)
-                if t0 == T_BANK and g >= 1:
-                    quantise_x(g - 1)
-        quantise_x(PASSES - 1)
+        load_mask_and_gcw(0)
 
         sign_of, rows_of, flip_of, grouped_of, codes_of, sums_of, prod_of, out_of = {}, {}, {}, {}, {}, {}, {}, {}
 
@@ -143,6 +114,11 @@ def tile_gcnfast_v_kernel(tc, h, e, AA_mask, GCW, GCB, z, grad_out, out):
                 if (r + Z_BUFS) % 2 == 0:
                     load_g((r + Z_BUFS) // 2)
                 load_z(r + Z_BUFS)
+            if r + 1 < MG_EARLY:
+                load_mask_and_gcw(r + 1)
+            if r + Z_BUFS == TILES - 1:
+                for late in range(MG_EARLY, TILES):
+                    load_mask_and_gcw(late)
 
         def positive(r, tau):
             nc.vector.tensor_scalar_max(
@@ -211,7 +187,7 @@ def tile_gcnfast_v_kernel(tc, h, e, AA_mask, GCW, GCB, z, grad_out, out):
                 sums_of[r].append(acc)
 
         def gate_product(r):
-            product = out_stage.tile([P, ROWS], BF16)
+            product = prod_stage.tile([P, ROWS], BF16)
             nc.vector.tensor_tensor(out=product[:], in0=mask_of[r][:], in1=gcw_of[r][:], op=ALU.mult)
             prod_of[r] = product
             if r + MG_BUFS < TILES:
@@ -231,16 +207,52 @@ def tile_gcnfast_v_kernel(tc, h, e, AA_mask, GCW, GCB, z, grad_out, out):
             cols = slice(n0 * N_COLS, n1 * N_COLS)
             nc.scalar.dma_start(out=out[r * P : (r + 1) * P, cols], in_=out_of[r][:, cols])
 
-        sign(0)
-        load_mask_and_gcw(3)
-        for tau in range(2):
-            positive(0, tau)
-        for tau in range(2):
-            mask_rows(0, tau)
-        sign(1)
+        x_codes = keep.tile([P, PASSES, ROWS], U32, align_bytes=64)
+        x_scales = keep.tile([P, PASSES, ROWS], U8, align_bytes=64)
+        x_grouped_of = {}
+
+        def quantise_x(g):
+            nc.vector.quantize_mx(
+                out=x_codes[:, g, :].bitcast(E4M3_X4),
+                scales=x_scales[:, g, :],
+                in_=x_grouped_of[g][:],
+            )
+
+        T_BANK = BANK // 2
+        for g in range(PASSES):
+            last = g == PASSES - 1
+            x_grouped = x_stage.tile([P, ROWS * PACK], BF16, align_bytes=64)
+            x_grouped_of[g] = x_grouped
+            if g >= 1:
+                quantise_x(g - 1)
+            if last:
+                sign(0)
+                sign(1)
+            for t0 in range(0, STEPS, T_BANK):
+                x_flip = flipped.tile([P, T_BANK, 2, P], BF16, tag="flip")
+                for tt in range(T_BANK):
+                    for ch in range(2):
+                        nc.tensor.transpose(x_flip[:, tt, ch, :], h_tiles[g][:, ch, t0 + tt, :], ident[:])
+                src = x_flip[:].rearrange("k t ch n -> k (t ch n)").bitcast(F32)
+                dst = x_grouped[:, t0 * NODES * PACK : (t0 + T_BANK) * NODES * PACK].bitcast(F32)
+                if (t0 // T_BANK) % 2 == 0 and not last:
+                    nc.scalar.copy(out=dst, in_=src)
+                else:
+                    nc.vector.tensor_copy(out=dst, in_=src)
+                if last and t0 == T_BANK:
+                    positive(0, 0)
+                if last and t0 == 2 * T_BANK:
+                    mask_rows(0, 0)
+        positive(0, 1)
+        mask_rows(0, 1)
+        quantise_x(PASSES - 1)
+
+
         for R in range(TILES + 2):
             if 1 <= R <= TILES:
                 quantise(R - 1)
+            if R >= 2:
+                gate_product(R - 2)
             if R < TILES:
                 flip(R, 0)
                 flip(R, 1)
@@ -265,7 +277,10 @@ def tile_gcnfast_v_kernel(tc, h, e, AA_mask, GCW, GCB, z, grad_out, out):
                 gate_out(R - 2, 1)
                 if R - 2 == TILES - 1:
                     store(R - 2, 1, 2)
-                else:
+                elif R - 2 >= TILES - 1 - STORE_LAG:
+                    if R - 2 == TILES - 1 - STORE_LAG:
+                        for held in range(R - 2 - STORE_LAG, R - 2):
+                            store(held, 0, 2)
                     store(R - 2, 0, 2)
-            if R < TILES:
-                gate_product(R)
+                elif R - 2 - STORE_LAG >= 0:
+                    store(R - 2 - STORE_LAG, 0, 2)

@@ -258,11 +258,11 @@ def tile_gcnfast_v_kernel(tc, h, e, AA_mask, GCW, GCB, z, grad_out, out):
                 flip(R, 1)
             if 1 <= R <= TILES:
                 multiply(R - 1)
-            if R + 2 < TILES:
-                sign(R + 2)
             if R < TILES:
                 regroup(R, 0)
                 regroup(R, 1)
+            if R + 2 < TILES:
+                sign(R + 2)
             if R + 1 < TILES:
                 positive(R + 1, 0)
                 positive(R + 1, 1)

import concourse.mybir as mybir
from concourse.masks import make_identity

F32 = mybir.dt.float32
BF16 = mybir.dt.bfloat16
U32 = mybir.dt.uint32
U8 = mybir.dt.uint8
E4M3_X4 = mybir.dt.float8_e4m3fn_x4
E5M2_X4 = mybir.dt.float8_e5m2_x4
ALU = mybir.AluOpType
ACT = mybir.ActivationFunctionType

P = 128
BATCH = 16
NODES = 64
STEPS = 16
FEAT = 128
ROWS = NODES * STEPS
PACK = 4
PASSES = BATCH // PACK
PAIRS = BATCH // 2
TILES = ROWS // P
N_COLS = 512
HALVES = ROWS // N_COLS
BANK = 8
Z_BUFS = 4
MG_BUFS = 8
MG_EARLY = 4
QUARTER = STEPS // 4
STORE_LAG = 2

FLOPS = 2 * ROWS * ROWS * BATCH * FEAT


def tile_gcnfast_v_kernel(tc, h, e, AA_mask, GCW, GCB, z, grad_out, out):
    nc = tc.nc

    with (
        tc.tile_pool(name="keep", bufs=1) as keep,
        tc.tile_pool(name="h_stage", bufs=PASSES) as h_stage,
        tc.tile_pool(name="x_stage", bufs=2) as x_stage,
        tc.tile_pool(name="z_stage", bufs=Z_BUFS) as z_stage,
        tc.tile_pool(name="mg_stage", bufs=MG_BUFS) as mg_stage,
        tc.tile_pool(name="dz_stage", bufs=2) as dz_stage,
        tc.tile_pool(name="prod_stage", bufs=3) as prod_stage,
        tc.tile_pool(name="out_stage", bufs=3 + STORE_LAG) as out_stage,
        tc.psum_pool(name="flipped", bufs=4) as flipped,
        tc.psum_pool(name="sums", bufs=4) as sums,
        tc.manual_schedule(),
    ):
        ident = keep.tile([P, P], BF16)
        make_identity(nc, ident[:])
        warm = keep.tile([P, 1], BF16)
        nc.scalar.activation(out=warm[:], in_=ident[:, 0:1], func=ACT.Sign)

        h_tiles = []
        for g in range(PASSES):
            h_g = h_stage.tile([P, 2, STEPS, FEAT], BF16)
            for bl in range(PACK):
                b = PACK * g + bl
                nc.sync.dma_start(
                    out=h_g[bl:P:PACK, :, :, :].rearrange("cl ch t d -> cl ch (t d)"),
                    in_=h[b : b + 1, :, :, :].rearrange("o (ch cl) t d -> cl (o ch) (t d)", ch=2),
                )
            h_tiles.append(h_g)

        g_of, z_of, mask_of, gcw_of = {}, {}, {}, {}

        def load_g(q):
            g_q = keep.tile([P, PAIRS, QUARTER, FEAT], BF16, name="g_q%d" % q)
            for b1 in range(2):
                nc.sync.dma_start(
                    out=g_q[b1:P:2, :, :, :].rearrange("s bh tq d -> s bh (tq d)"),
                    in_=grad_out[b1:BATCH:2, :, q * QUARTER : (q + 1) * QUARTER, :].rearrange(
                        "bh s tq d -> s bh (tq d)"
                    ),
                )
            g_of[q] = g_q

        def load_z(r):
            z_t = z_stage.tile([P, 2, PAIRS, FEAT], F32)
            for tau in range(2):
                i0 = (2 * r + tau) * NODES
                for b1 in range(2):
                    nc.sync.dma_start(
                        out=z_t[b1:P:2, tau, :, :],
                        in_=z[b1:BATCH:2, i0 : i0 + NODES, :].rearrange("bh s d -> s bh d"),
                    )
            z_of[r] = z_t

        def load_mask_and_gcw(r):
            mask_t = mg_stage.tile([P, ROWS], BF16)
            gcw_t = mg_stage.tile([P, ROWS], BF16)
            nc.sync.dma_start(out=mask_t[:], in_=AA_mask[r * P : (r + 1) * P, :])
            nc.sync.dma_start(out=gcw_t[:], in_=GCW[r * P : (r + 1) * P, :])
            mask_of[r], gcw_of[r] = mask_t, gcw_t

        load_g(0)
        load_z(0)
        load_z(1)
        load_g(1)
        load_z(2)
        load_z(3)
        load_mask_and_gcw(0)

        sign_of, rows_of, flip_of, grouped_of, codes_of, sums_of, prod_of, out_of = {}, {}, {}, {}, {}, {}, {}, {}

        def sign(r):
            sign_t = dz_stage.tile([P, 2, PAIRS, FEAT], BF16)
            sign_of[r] = sign_t
            for tau in range(2):
                nc.scalar.activation(out=sign_t[:, tau, :, :], in_=z_of[r][:, tau, :, :], func=ACT.Sign)
            if r + Z_BUFS < TILES:
                if (r + Z_BUFS) % 2 == 0:
                    load_g((r + Z_BUFS) // 2)
                load_z(r + Z_BUFS)
            if r + 1 < MG_EARLY:
                load_mask_and_gcw(r + 1)
            if r + Z_BUFS == TILES - 1:
                for late in range(MG_EARLY, TILES):
                    load_mask_and_gcw(late)

        def positive(r, tau):
            nc.vector.tensor_scalar_max(
                out=sign_of[r][:, tau, :, :], in0=sign_of[r][:, tau, :, :], scalar1=0.0
            )

        def mask_rows(r, tau):
            if tau == 0:
                dz_rows = dz_stage.tile([P, 2, PAIRS, FEAT], BF16)
                rows_of[r] = dz_rows
            nc.vector.tensor_tensor(
                out=rows_of[r][:, tau, :, :],
                in0=sign_of[r][:, tau, :, :],
                in1=g_of[r // 2][:, :, 2 * (r % 2) + tau, :],
                op=ALU.mult,
            )

        def flip(r, tau):
            dz_flip = flipped.tile([P, PAIRS, P], BF16, tag="flip")
            for bh in range(PAIRS):
                nc.tensor.transpose(dz_flip[:, bh, :], rows_of[r][:, tau, bh, :], ident[:])
            flip_of[(r, tau)] = dz_flip

        def regroup(r, tau):
            if tau == 0:
                dz_grouped = dz_stage.tile([P, PASSES, P * PACK], BF16, align_bytes=64)
                grouped_of[r] = dz_grouped
            words = NODES * 2
            nc.scalar.copy(
                out=grouped_of[r][:]
                .bitcast(F32)[:, :, tau * words : (tau + 1) * words]
                .rearrange("k g (s b2) -> k g s b2", b2=2),
                in_=flip_of[(r, tau)][:]
                .rearrange("k bh n -> k (bh n)")
                .bitcast(F32)
                .rearrange("k (g b2 s) -> k g s b2", g=PASSES, b2=2),
            )

        def quantise(r):
            dz_codes = dz_stage.tile([P, PASSES * P], U32, align_bytes=64)
            dz_scales = dz_stage.tile([P, PASSES * P], U8, align_bytes=64)
            nc.vector.quantize_mx(
                out=dz_codes[:].bitcast(E5M2_X4),
                scales=dz_scales[:],
                in_=grouped_of[r][:].rearrange("k g m -> k (g m)"),
            )
            codes_of[r] = (dz_codes, dz_scales)

        def multiply(r):
            dz_codes, dz_scales = codes_of[r]
            sums_of[r] = []
            for n in range(HALVES):
                cols = slice(n * N_COLS, (n + 1) * N_COLS)
                acc = sums.tile([P, N_COLS], F32)
                for g in range(PASSES):
                    m_cols = slice(g * P, (g + 1) * P)
                    nc.tensor.matmul_mx(
                        out=acc[:],
                        lhsT=dz_codes[:, m_cols].bitcast(E5M2_X4),
                        lhsT_scale=dz_scales[:, m_cols],
                        rhs=x_codes[:, g, cols].bitcast(E4M3_X4),
                        rhs_scale=x_scales[:, g, cols],
                        start=(g == 0),
                        stop=(g == PASSES - 1),
                    )
                sums_of[r].append(acc)

        def gate_product(r):
            product = prod_stage.tile([P, ROWS], BF16)
            nc.vector.tensor_tensor(out=product[:], in0=mask_of[r][:], in1=gcw_of[r][:], op=ALU.mult)
            prod_of[r] = product
            if r + MG_BUFS < TILES:
                load_mask_and_gcw(r + MG_BUFS)

        def gate_out(r, n):
            if n == 0:
                out_t = out_stage.tile([P, ROWS], F32)
                out_of[r] = out_t
            cols = slice(n * N_COLS, (n + 1) * N_COLS)
            nc.vector.scalar_tensor_tensor(
                out=out_of[r][:, cols], in0=prod_of[r][:, cols], scalar=0.0, in1=sums_of[r][n][:],
                op0=ALU.is_gt, op1=ALU.mult,
            )

        def store(r, n0, n1):
            cols = slice(n0 * N_COLS, n1 * N_COLS)
            nc.scalar.dma_start(out=out[r * P : (r + 1) * P, cols], in_=out_of[r][:, cols])

        x_codes = keep.tile([P, PASSES, ROWS], U32, align_bytes=64)
        x_scales = keep.tile([P, PASSES, ROWS], U8, align_bytes=64)
        x_grouped_of = {}

        def quantise_x(g):
            nc.vector.quantize_mx(
                out=x_codes[:, g, :].bitcast(E4M3_X4),
                scales=x_scales[:, g, :],
                in_=x_grouped_of[g][:],
            )

        T_BANK = BANK // 2
        for g in range(PASSES):
            last = g == PASSES - 1
            x_grouped = x_stage.tile([P, ROWS * PACK], BF16, align_bytes=64)
            x_grouped_of[g] = x_grouped
            if g >= 1:
                quantise_x(g - 1)
            if last:
                sign(0)
                sign(1)
            for t0 in range(0, STEPS, T_BANK):
                x_flip = flipped.tile([P, T_BANK, 2, P], BF16, tag="flip")
                for tt in range(T_BANK):
                    for ch in range(2):
                        nc.tensor.transpose(x_flip[:, tt, ch, :], h_tiles[g][:, ch, t0 + tt, :], ident[:])
                src = x_flip[:].rearrange("k t ch n -> k (t ch n)").bitcast(F32)
                dst = x_grouped[:, t0 * NODES * PACK : (t0 + T_BANK) * NODES * PACK].bitcast(F32)
                if (t0 // T_BANK) % 2 == 0 and not last:
                    nc.scalar.copy(out=dst, in_=src)
                else:
                    nc.vector.tensor_copy(out=dst, in_=src)
                if last and t0 == T_BANK:
                    positive(0, 0)
                if last and t0 == 2 * T_BANK:
                    mask_rows(0, 0)
        positive(0, 1)
        mask_rows(0, 1)
        quantise_x(PASSES - 1)


        for R in range(TILES + 2):
            if 1 <= R <= TILES:
                quantise(R - 1)
            if R >= 2:
                gate_product(R - 2)
            if R < TILES:
                flip(R, 0)
                flip(R, 1)
            if 1 <= R <= TILES:
                multiply(R - 1)
            if R < TILES:
                regroup(R, 0)
                regroup(R, 1)
            if R + 2 < TILES:
                sign(R + 2)
            if R + 1 < TILES:
                positive(R + 1, 0)
                positive(R + 1, 1)
            if R >= 2:
                gate_out(R - 2, 0)
                if R - 2 == TILES - 1:
                    store(R - 2, 0, 1)
            if R + 1 < TILES:
                mask_rows(R + 1, 0)
                mask_rows(R + 1, 1)
            if R >= 2:
                gate_out(R - 2, 1)
                if R - 2 == TILES - 1:
                    store(R - 2, 1, 2)
                elif R - 2 >= TILES - 1 - STORE_LAG:
                    if R - 2 == TILES - 1 - STORE_LAG:
                        for held in range(R - 2 - STORE_LAG, R - 2):
                            store(held, 0, 2)
                    store(R - 2, 0, 2)
                elif R - 2 - STORE_LAG >= 0:
                    store(R - 2 - STORE_LAG, 0, 2)
